import numpy as np
import ml_dtypes


def mxq(x, axis, fmt="e4m3"):
    dtype, down = {"e4m3": (ml_dtypes.float8_e4m3fn, 7), "e5m2": (ml_dtypes.float8_e5m2, 14)}[fmt]
    v = np.moveaxis(np.asarray(x, np.float32).astype(ml_dtypes.bfloat16).astype(np.float64), axis, -1)
    blocks = v.reshape(v.shape[:-1] + (-1, 32))
    amax = np.abs(blocks).max(-1, keepdims=True)
    byte = np.maximum(np.where(amax > 0, np.frexp(amax)[1] - 1 + 127, 0) - down, 1)
    scale = np.exp2(byte - 127.0)
    codes = (blocks / scale).astype(np.float32).astype(dtype).astype(np.float64)
    return np.moveaxis((codes * scale).reshape(v.shape), -1, axis)


WIDE = False


def mx_kscale(k):
    if not WIDE:
        return np.ones(k)
    levels = np.array([10, -10, 5, -5, 0])
    a = np.random.permutation(np.resize(levels, k // 512 * 4)).reshape(k // 512, 4)
    idx = np.arange(k)
    return np.exp2(a[idx // 512, idx % 128 // 32])


BF16 = ml_dtypes.bfloat16


def bf(x):
    return np.asarray(x, np.float32).astype(BF16)


def f64(x):
    return np.asarray(x).astype(np.float64)


B, H, A = 512, 1024, 1024


def setup_inputs():
    s = mx_kscale(H)
    return {
        "x": bf(np.random.standard_normal((B, H)) * s),
        "alpha": bf(np.random.standard_normal((B, H)) * s),
        "aa": bf(np.random.standard_normal((B, A)) * 0.5),
        "bb": bf(np.random.uniform(0.5, 1.5, (B, A))),
        "pp": bf(np.random.standard_normal((B, A))),
        "time_decay": bf(-1.0 + 1.5 * np.random.standard_normal(A)),
        "time_first": bf(-1.2 + 0.5 * np.random.standard_normal(A)),
        "time_mix_k": bf(np.random.uniform(0.1, 0.9, H)),
        "time_mix_v": bf(np.random.uniform(0.2, 1.1, H)),
        "Wk": bf(np.random.standard_normal((A, H)) * 1.5 / np.sqrt(H) / s),
        "Wv": bf(np.random.standard_normal((A, H)) * 1.2 / np.sqrt(H) / s),
    }


def reference(x, alpha, aa, bb, pp, time_decay, time_first, time_mix_k, time_mix_v, Wk, Wv):
    x, alpha, aa, bb, pp = f64(x), f64(alpha), f64(aa), f64(bb), f64(pp)
    time_decay, time_first = f64(time_decay), f64(time_first)
    time_mix_k, time_mix_v = f64(time_mix_k), f64(time_mix_v)
    xk = x * time_mix_k + alpha * (1.0 - time_mix_k)
    xv = x * time_mix_v + alpha * (1.0 - time_mix_v)
    k = mxq(xk, 1, "e4m3") @ mxq(f64(Wk), 1, "e4m3").T
    v = mxq(xv, 1, "e4m3") @ mxq(f64(Wv), 1, "e4m3").T
    ww = time_first + k
    qq = np.maximum(pp, ww)
    e1 = np.exp(pp - qq)
    e2 = np.exp(ww - qq)
    wkv = (e1 * aa + e2 * v) / (e1 * bb + e2)
    ww2 = pp + time_decay
    qq2 = np.maximum(ww2, k)
    e1b = np.exp(ww2 - qq2)
    e2b = np.exp(k - qq2)
    next_aa = e1b * aa + e2b * v
    next_bb = e1b * bb + e2b
    return (wkv, next_aa, next_bb, qq2)

@@ -1,0 +1,285 @@
+from contextlib import ExitStack
+
+import concourse.mybir as mybir
+from concourse.masks import make_identity
+
+F32 = mybir.dt.float32
+BF16 = mybir.dt.bfloat16
+U32 = mybir.dt.uint32
+U8 = mybir.dt.uint8
+FP8X4 = mybir.dt.float8_e4m3fn_x4
+ALU = mybir.AluOpType
+ACT = mybir.ActivationFunctionType
+
+B, H, A = 512, 1024, 1024
+P = 128
+ROW_TILES = B // P
+K_PASS = 4 * P
+PASSES = H // K_PASS
+N_TILE = 512
+COL_TILES = A // N_TILE
+PAIR_COLS = 2 * P
+PAIR_BLOCKS = H // PAIR_COLS
+TINY = 2.0 ** -60
+
+FLOPS = 2 * 2 * B * H * A
+
+
+def tile_rwkvtimemix_pa_kernel(
+    tc, x, alpha, aa, bb, pp, time_decay, time_first, time_mix_k, time_mix_v, Wk, Wv,
+    out_0, out_1, out_2, out_3,
+):
+    nc = tc.nc
+    with ExitStack() as stack:
+        const = stack.enter_context(tc.tile_pool(name="const", bufs=1))
+        keep = stack.enter_context(tc.tile_pool(name="keep", bufs=1))
+        weights = stack.enter_context(tc.tile_pool(name="weights", bufs=4))
+        turned = stack.enter_context(tc.psum_pool(name="turned", bufs=4))
+        sums = stack.enter_context(tc.psum_pool(name="sums", bufs=2))
+
+        def rows_on_partitions(dram):
+            return dram.rearrange("(r p) n -> p r n", p=P)
+
+        def as_one_row(vector):
+            return vector.rearrange("(o c) -> o c", o=1)
+
+        mix_rows = const.tile([P, PAIR_COLS], BF16)
+        nc.vector.memset(mix_rows[:], 0.0)
+        nc.scalar.dma_start(out=mix_rows[0:4, :], in_=time_mix_k.rearrange("(j c) -> j c", c=PAIR_COLS))
+        nc.scalar.dma_start(out=mix_rows[4:8, :], in_=time_mix_v.rearrange("(j c) -> j c", c=PAIR_COLS))
+        vec_rows = const.tile([P, 2 * A], BF16)
+        nc.vector.memset(vec_rows[:], 0.0)
+        nc.scalar.dma_start(out=vec_rows[0:1, 0:A], in_=as_one_row(time_first))
+        nc.scalar.dma_start(out=vec_rows[1:2, 0:A], in_=as_one_row(time_decay))
+        nc.scalar.dma_start(out=vec_rows[0:1, A : 2 * A], in_=as_one_row(time_decay))
+
+        identity = const.tile([P, P], F32)
+        make_identity(nc, identity[:])
+        ones = const.tile([P, P], BF16)
+        nc.vector.memset(ones[:], 1.0)
+        tiny = const.tile([P, 1], F32)
+        nc.vector.memset(tiny[:], TINY)
+        mix = const.tile([P, 4 * PAIR_BLOCKS], F32)
+        one_minus_mix = const.tile([P, 4 * PAIR_BLOCKS], F32)
+        spread = const.tile([P, 2 * A], F32)
+
+        xk_words = keep.tile([P, PASSES, B], U32, align_bytes=64)
+        xk_scales = keep.tile([P, PASSES, B], U8, align_bytes=64)
+        xv_words = keep.tile([P, PASSES, B], U32, align_bytes=64)
+        xv_scales = keep.tile([P, PASSES, B], U8, align_bytes=64)
+        wk_words = keep.tile([P, COL_TILES, PASSES, N_TILE], U32, align_bytes=64)
+        wk_scales = keep.tile([P, COL_TILES, PASSES, N_TILE], U8, align_bytes=64)
+        wv_words = keep.tile([P, COL_TILES, PASSES, N_TILE], U32, align_bytes=64)
+        wv_scales = keep.tile([P, COL_TILES, PASSES, N_TILE], U8, align_bytes=64)
+
+        aa_sb = keep.tile([P, ROW_TILES, A], BF16)
+        bb_sb = keep.tile([P, ROW_TILES, A], BF16)
+        pp_sb = keep.tile([P, ROW_TILES, A], BF16)
+        log_shift = []
+        rho = []
+        decayed = []
+        for c in range(COL_TILES):
+            log_shift.append(keep.tile([P, ROW_TILES, N_TILE], F32, name="log_shift%d" % c))
+            rho.append(keep.tile([P, ROW_TILES, N_TILE], F32, name="rho%d" % c))
+            decayed.append(keep.tile([P, ROW_TILES, N_TILE], F32, name="decayed%d" % c))
+
+        def load_weight_half(w, c):
+            w_sb = weights.tile([P, N_TILE // P, H], BF16, tag="w_sb")
+            nc.sync.dma_start(out=w_sb[:], in_=rows_on_partitions(w[c * N_TILE : (c + 1) * N_TILE, :]))
+            return w_sb
+
+        def quantise_weight_half(w_sb, words, scales, c):
+            for g in range(PASSES):
+                grouped = weights.tile([P, 4 * N_TILE], BF16, tag="w_grouped", align_bytes=64)
+                grouped_pairs = grouped[:].bitcast(F32).rearrange("p (a u) -> p a u", u=2)
+                for half in range(2):
+                    w_turned = turned.tile([P, 2, 2 * P], F32, tag="turned")
+                    for u in range(2):
+                        for i in range(2):
+                            block = w_sb[:, 2 * half + i, :].bitcast(F32)
+                            j = 2 * g + u
+                            nc.tensor.transpose(
+                                w_turned[:, u, i * P : (i + 1) * P], block[:, j * P : (j + 1) * P], identity[:]
+                            )
+                    nc.scalar.copy(
+                        out=grouped_pairs[:, half * 2 * P : (half + 1) * 2 * P, :],
+                        in_=w_turned[:].rearrange("p u a -> p a u"),
+                    )
+                nc.vector.quantize_mx(
+                    out=words[:, c, g, :].bitcast(FP8X4), scales=scales[:, c, g, :], in_=grouped[:]
+                )
+
+        def logarithm_of_bb(c):
+            cols = slice(c * N_TILE, (c + 1) * N_TILE)
+            nc.scalar.activation(out=log_shift[c][:], in_=bb_sb[:, :, cols], func=ACT.Ln, bias=tiny[:])
+
+        def reciprocal_of_bb(c):
+            nc.scalar.activation(out=rho[c][:], in_=log_shift[c][:], func=ACT.Exp, scale=-1.0)
+
+        with tc.tile_pool(name="front", bufs=1) as front:
+            x_sb = front.tile([P, ROW_TILES, H], BF16)
+            alpha_sb = front.tile([P, ROW_TILES, H], BF16)
+            nc.sync.dma_start(out=bb_sb[:, :, 0:N_TILE], in_=rows_on_partitions(bb)[:, :, 0:N_TILE])
+            for g in range(PASSES):
+                h_cols = slice(g * K_PASS, (g + 1) * K_PASS)
+                nc.sync.dma_start(out=x_sb[:, :, h_cols], in_=rows_on_partitions(x)[:, :, h_cols])
+                nc.sync.dma_start(out=alpha_sb[:, :, h_cols], in_=rows_on_partitions(alpha)[:, :, h_cols])
+            nc.sync.dma_start(out=pp_sb[:], in_=rows_on_partitions(pp))
+            nc.sync.dma_start(out=bb_sb[:, :, N_TILE:A], in_=rows_on_partitions(bb)[:, :, N_TILE:A])
+            wk_sb = [load_weight_half(Wk, 0)]
+            wv_sb = [load_weight_half(Wv, 0)]
+            nc.sync.dma_start(out=aa_sb[:], in_=rows_on_partitions(aa))
+            wk_sb.append(load_weight_half(Wk, 1))
+            wv_sb.append(load_weight_half(Wv, 1))
+
+            logarithm_of_bb(0)
+
+            mix_turned = turned.tile([P, P], F32, tag="turned")
+            nc.tensor.transpose(mix_turned[:], mix_rows[:].bitcast(F32), identity[:])
+            nc.vector.tensor_copy(out=mix[:], in_=mix_turned[:, 0 : 2 * PAIR_BLOCKS].bitcast(BF16))
+            nc.vector.tensor_scalar(
+                out=one_minus_mix[:], in0=mix[:], scalar1=-1.0, scalar2=1.0, op0=ALU.mult, op1=ALU.add
+            )
+
+            for i in range(2 * A // N_TILE):
+                cols = slice(i * N_TILE, (i + 1) * N_TILE)
+                spread_ps = turned.tile([P, N_TILE], F32, tag="turned")
+                nc.tensor.matmul(out=spread_ps[:], lhsT=ones[:], rhs=vec_rows[:, cols], start=True, stop=True)
+                nc.vector.tensor_copy(out=spread[:, cols], in_=spread_ps[:])
+
+            xk_mixed = front.tile([P, PASSES, 4, B], BF16)
+            xv_mixed = front.tile([P, PASSES, 4, B], BF16)
+            for j in range(PAIR_BLOCKS):
+                g, u = divmod(j, 2)
+                x_turned = turned.tile([P, B], F32, tag="turned")
+                alpha_turned = turned.tile([P, B], F32, tag="turned")
+                for r in range(ROW_TILES):
+                    rows = slice(r * P, (r + 1) * P)
+                    pair_cols = slice(j * P, (j + 1) * P)
+                    nc.tensor.transpose(x_turned[:, rows], x_sb[:, r, :].bitcast(F32)[:, pair_cols], identity[:])
+                    nc.tensor.transpose(
+                        alpha_turned[:, rows], alpha_sb[:, r, :].bitcast(F32)[:, pair_cols], identity[:]
+                    )
+                x_pairs = x_turned[:].bitcast(BF16).rearrange("p (b e) -> p b e", e=2)
+                alpha_pairs = alpha_turned[:].bitcast(BF16).rearrange("p (b e) -> p b e", e=2)
+                for e in range(2):
+                    for first_col, mixed in ((0, xk_mixed), (2 * PAIR_BLOCKS, xv_mixed)):
+                        col = first_col + 2 * j + e
+                        alpha_part = front.tile([P, B], F32, tag="alpha_part", bufs=4)
+                        nc.scalar.activation(
+                            out=alpha_part[:], in_=alpha_pairs[:, :, e], func=ACT.Copy,
+                            scale=one_minus_mix[:, col : col + 1],
+                        )
+                        nc.vector.scalar_tensor_tensor(
+                            out=mixed[:, g, 2 * u + e, :], in0=x_pairs[:, :, e], scalar=mix[:, col : col + 1],
+                            in1=alpha_part[:], op0=ALU.mult, op1=ALU.add,
+                        )
+
+            xk_grouped = front.tile([P, PASSES, B, 4], BF16, align_bytes=64)
+            xv_grouped = front.tile([P, PASSES, B, 4], BF16, align_bytes=64)
+            for g in range(PASSES):
+                for mixed, grouped in ((xk_mixed, xk_grouped), (xv_mixed, xv_grouped)):
+                    nc.vector.tensor_copy(
+                        out=grouped[:, g].rearrange("p (c i) t -> p c t i", i=4),
+                        in_=mixed[:, g].rearrange("p t (c i) -> p c t i", i=4),
+                    )
+            for g in range(PASSES):
+                for grouped, words, scales in (
+                    (xk_grouped, xk_words, xk_scales), (xv_grouped, xv_words, xv_scales),
+                ):
+                    nc.vector.quantize_mx(
+                        out=words[:, g, :].bitcast(FP8X4), scales=scales[:, g, :],
+                        in_=grouped[:, g].rearrange("p b t -> p (b t)"),
+                    )
+
+        logarithm_of_bb(1)
+        reciprocal_of_bb(0)
+
+        def prepare_state(c):
+            cols = slice(c * N_TILE, (c + 1) * N_TILE)
+            for r in range(ROW_TILES):
+                nc.gpsimd.tensor_tensor(
+                    out=decayed[c][:, r, :], in0=pp_sb[:, r, cols], in1=spread[:, A + c * N_TILE : A + (c + 1) * N_TILE],
+                    op=ALU.add,
+                )
+            for r in range(ROW_TILES):
+                nc.gpsimd.tensor_tensor(
+                    out=log_shift[c][:, r, :], in0=log_shift[c][:, r, :], in1=spread[:, cols], op=ALU.subtract
+                )
+                nc.gpsimd.tensor_tensor(out=rho[c][:, r, :], in0=aa_sb[:, r, cols], in1=rho[c][:, r, :], op=ALU.mult)
+
+        with tc.tile_pool(name="late", bufs=3) as late:
+
+            def project(c, r, x_words, x_scales, w_words, w_scales, tag):
+                acc = sums.tile([P, N_TILE], F32, tag=tag)
+                rows = slice(r * P, (r + 1) * P)
+                for g in range(PASSES):
+                    nc.tensor.matmul_mx(
+                        out=acc[:],
+                        lhsT=x_words[:, g, rows].bitcast(FP8X4), lhsT_scale=x_scales[:, g, rows],
+                        rhs=w_words[:, c, g, :].bitcast(FP8X4), rhs_scale=w_scales[:, c, g, :],
+                        start=(g == 0), stop=(g == PASSES - 1),
+                    )
+                return acc
+
+            def output_tile(c, r):
+                rows = slice(r * P, (r + 1) * P)
+                cols = slice(c * N_TILE, (c + 1) * N_TILE)
+                k_ps = project(c, r, xk_words, xk_scales, wk_words, wk_scales, "k")
+                v_ps = project(c, r, xv_words, xv_scales, wv_words, wv_scales, "v")
+
+                d2 = late.tile([P, N_TILE], F32, tag="d2")
+                nc.vector.tensor_tensor(out=d2[:], in0=k_ps[:], in1=decayed[c][:, r, :], op=ALU.subtract)
+                qq2 = late.tile([P, N_TILE], F32, tag="qq2")
+                nc.vector.tensor_tensor(out=qq2[:], in0=k_ps[:], in1=decayed[c][:, r, :], op=ALU.max)
+                nc.sync.dma_start(out=out_3[rows, cols], in_=qq2[:])
+                wkv = late.tile([P, N_TILE], F32, tag="wkv")
+                nc.vector.tensor_tensor(out=wkv[:], in0=v_ps[:], in1=rho[c][:, r, :], op=ALU.subtract)
+                gate = late.tile([P, N_TILE], F32, tag="gate")
+                nc.vector.tensor_tensor(out=gate[:], in0=d2[:], in1=log_shift[c][:, r, :], op=ALU.subtract)
+
+                grow_old = late.tile([P, N_TILE], F32, tag="grow_old")
+                nc.scalar.activation(out=grow_old[:], in_=d2[:], func=ACT.Exp, scale=-1.0)
+                grow_new = late.tile([P, N_TILE], F32, tag="grow_new")
+                nc.scalar.activation(out=grow_new[:], in_=d2[:], func=ACT.Exp)
+                nc.scalar.activation(out=gate[:], in_=gate[:], func=ACT.Tanh, scale=0.5)
+
+                new_part = late.tile([P, N_TILE], F32, tag="new_part")
+                nc.vector.scalar_tensor_tensor(
+                    out=new_part[:], in0=grow_new[:], scalar=1.0, in1=v_ps[:], op0=ALU.min, op1=ALU.mult
+                )
+                next_aa = late.tile([P, N_TILE], F32, tag="next_aa")
+                nc.vector.scalar_tensor_tensor(
+                    out=next_aa[:], in0=grow_old[:], scalar=1.0, in1=aa_sb[:, r, cols], op0=ALU.min, op1=ALU.mult
+                )
+                next_bb = late.tile([P, N_TILE], F32, tag="next_bb")
+                nc.vector.scalar_tensor_tensor(
+                    out=next_bb[:], in0=grow_old[:], scalar=1.0, in1=bb_sb[:, r, cols], op0=ALU.min, op1=ALU.mult
+                )
+                nc.vector.scalar_tensor_tensor(
+                    out=wkv[:], in0=gate[:], scalar=1.0, in1=wkv[:], op0=ALU.add, op1=ALU.mult
+                )
+                nc.vector.tensor_tensor(out=next_aa[:], in0=next_aa[:], in1=new_part[:], op=ALU.add)
+                nc.sync.dma_start(out=out_1[rows, cols], in_=next_aa[:])
+                nc.vector.scalar_tensor_tensor(
+                    out=next_bb[:], in0=grow_new[:], scalar=1.0, in1=next_bb[:], op0=ALU.min, op1=ALU.add
+                )
+                nc.sync.dma_start(out=out_2[rows, cols], in_=next_bb[:])
+                nc.vector.scalar_tensor_tensor(
+                    out=wkv[:], in0=wkv[:], scalar=0.5, in1=rho[c][:, r, :], op0=ALU.mult, op1=ALU.add
+                )
+                nc.sync.dma_start(out=out_0[rows, cols], in_=wkv[:])
+
+            def prepare_column_tile(c):
+                prepare_state(c)
+                quantise_weight_half(wk_sb[c], wk_words, wk_scales, c)
+                quantise_weight_half(wv_sb[c], wv_words, wv_scales, c)
+
+            prepare_column_tile(0)
+            reciprocal_of_bb(1)
+            for r in range(ROW_TILES):
+                output_tile(0, r)
+                if r == ROW_TILES // 2 - 1:
+                    prepare_column_tile(1)
+            for r in range(ROW_TILES):
+                output_tile(1, r)

@@ -43,6 +43,9 @@ def tile_rwkvtimemix_pa_kernel(
         def as_one_row(vector):
             return vector.rearrange("(o c) -> o c", o=1)
 
+        def channels(c):
+            return slice(c * N_TILE, (c + 1) * N_TILE)
+
         mix_rows = const.tile([P, PAIR_COLS], BF16)
         nc.vector.memset(mix_rows[:], 0.0)
         nc.scalar.dma_start(out=mix_rows[0:4, :], in_=time_mix_k.rearrange("(j c) -> j c", c=PAIR_COLS))
@@ -61,7 +64,8 @@ def tile_rwkvtimemix_pa_kernel(
         nc.vector.memset(tiny[:], TINY)
         mix = const.tile([P, 4 * PAIR_BLOCKS], F32)
         one_minus_mix = const.tile([P, 4 * PAIR_BLOCKS], F32)
-        spread = const.tile([P, 2 * A], F32)
+        first_plus_decay = const.tile([P, A], F32)
+        decay = const.tile([P, A], F32)
 
         xk_words = keep.tile([P, PASSES, B], U32, align_bytes=64)
         xk_scales = keep.tile([P, PASSES, B], U8, align_bytes=64)
@@ -83,14 +87,17 @@ def tile_rwkvtimemix_pa_kernel(
             rho.append(keep.tile([P, ROW_TILES, N_TILE], F32, name="rho%d" % c))
             decayed.append(keep.tile([P, ROW_TILES, N_TILE], F32, name="decayed%d" % c))
 
+        def load_state_half(state_sb, state, c):
+            nc.sync.dma_start(out=state_sb[:, :, channels(c)], in_=rows_on_partitions(state)[:, :, channels(c)])
+
         def load_weight_half(w, c):
             w_sb = weights.tile([P, N_TILE // P, H], BF16, tag="w_sb")
-            nc.sync.dma_start(out=w_sb[:], in_=rows_on_partitions(w[c * N_TILE : (c + 1) * N_TILE, :]))
+            nc.sync.dma_start(out=w_sb[:], in_=rows_on_partitions(w[channels(c), :]))
             return w_sb
 
         def quantise_weight_half(w_sb, words, scales, c):
             for g in range(PASSES):
-                grouped = weights.tile([P, 4 * N_TILE], BF16, tag="w_grouped", align_bytes=64)
+                grouped = weights.tile([P, 4 * N_TILE], BF16, tag="w_grouped", bufs=2, align_bytes=64)
                 grouped_pairs = grouped[:].bitcast(F32).rearrange("p (a u) -> p a u", u=2)
                 for half in range(2):
                     w_turned = turned.tile([P, 2, 2 * P], F32, tag="turned")
@@ -109,30 +116,57 @@ def tile_rwkvtimemix_pa_kernel(
                     out=words[:, c, g, :].bitcast(FP8X4), scales=scales[:, c, g, :], in_=grouped[:]
                 )
 
-        def logarithm_of_bb(c):
-            cols = slice(c * N_TILE, (c + 1) * N_TILE)
-            nc.scalar.activation(out=log_shift[c][:], in_=bb_sb[:, :, cols], func=ACT.Ln, bias=tiny[:])
+        def logarithm_and_reciprocal_of_bb(c):
+            log_bb = keep.tile([P, ROW_TILES, N_TILE], F32, tag="log_bb")
+            nc.scalar.activation(out=log_bb[:], in_=bb_sb[:, :, channels(c)], func=ACT.Ln, bias=tiny[:])
+            nc.scalar.activation(out=rho[c][:], in_=log_bb[:], func=ACT.Exp, scale=-1.0)
+            return log_bb
 
-        def reciprocal_of_bb(c):
-            nc.scalar.activation(out=rho[c][:], in_=log_shift[c][:], func=ACT.Exp, scale=-1.0)
+        def decay_pp(engine, c):
+            for r in range(ROW_TILES):
+                engine.tensor_tensor(
+                    out=decayed[c][:, r, :], in0=pp_sb[:, r, channels(c)], in1=decay[:, channels(c)], op=ALU.add
+                )
+
+        def shift_logarithm(engine, c, log_bb):
+            for r in range(ROW_TILES):
+                engine.tensor_tensor(
+                    out=log_shift[c][:, r, :], in0=log_bb[:, r, :], in1=first_plus_decay[:, channels(c)],
+                    op=ALU.subtract,
+                )
+
+        def old_average(engine, c):
+            for r in range(ROW_TILES):
+                engine.tensor_tensor(
+                    out=rho[c][:, r, :], in0=aa_sb[:, r, channels(c)], in1=rho[c][:, r, :], op=ALU.mult
+                )
 
         with tc.tile_pool(name="front", bufs=1) as front:
             x_sb = front.tile([P, ROW_TILES, H], BF16)
             alpha_sb = front.tile([P, ROW_TILES, H], BF16)
-            nc.sync.dma_start(out=bb_sb[:, :, 0:N_TILE], in_=rows_on_partitions(bb)[:, :, 0:N_TILE])
+            load_state_half(bb_sb, bb, 0)
+            load_state_half(pp_sb, pp, 0)
             for g in range(PASSES):
                 h_cols = slice(g * K_PASS, (g + 1) * K_PASS)
                 nc.sync.dma_start(out=x_sb[:, :, h_cols], in_=rows_on_partitions(x)[:, :, h_cols])
                 nc.sync.dma_start(out=alpha_sb[:, :, h_cols], in_=rows_on_partitions(alpha)[:, :, h_cols])
-            nc.sync.dma_start(out=pp_sb[:], in_=rows_on_partitions(pp))
-            nc.sync.dma_start(out=bb_sb[:, :, N_TILE:A], in_=rows_on_partitions(bb)[:, :, N_TILE:A])
+            load_state_half(aa_sb, aa, 0)
             wk_sb = [load_weight_half(Wk, 0)]
             wv_sb = [load_weight_half(Wv, 0)]
-            nc.sync.dma_start(out=aa_sb[:], in_=rows_on_partitions(aa))
+            load_state_half(bb_sb, bb, 1)
+            load_state_half(pp_sb, pp, 1)
+            load_state_half(aa_sb, aa, 1)
             wk_sb.append(load_weight_half(Wk, 1))
             wv_sb.append(load_weight_half(Wv, 1))
 
-            logarithm_of_bb(0)
+            for c in range(COL_TILES):
+                for first_col, repeated in ((A, decay), (0, first_plus_decay)):
+                    repeated_ps = turned.tile([P, N_TILE], F32, tag="turned")
+                    nc.tensor.matmul(
+                        out=repeated_ps[:], lhsT=ones[:],
+                        rhs=vec_rows[:, first_col + c * N_TILE : first_col + (c + 1) * N_TILE], start=True, stop=True,
+                    )
+                    nc.vector.tensor_copy(out=repeated[:, channels(c)], in_=repeated_ps[:])
 
             mix_turned = turned.tile([P, P], F32, tag="turned")
             nc.tensor.transpose(mix_turned[:], mix_rows[:].bitcast(F32), identity[:])
@@ -141,11 +175,10 @@ def tile_rwkvtimemix_pa_kernel(
                 out=one_minus_mix[:], in0=mix[:], scalar1=-1.0, scalar2=1.0, op0=ALU.mult, op1=ALU.add
             )
 
-            for i in range(2 * A // N_TILE):
-                cols = slice(i * N_TILE, (i + 1) * N_TILE)
-                spread_ps = turned.tile([P, N_TILE], F32, tag="turned")
-                nc.tensor.matmul(out=spread_ps[:], lhsT=ones[:], rhs=vec_rows[:, cols], start=True, stop=True)
-                nc.vector.tensor_copy(out=spread[:, cols], in_=spread_ps[:])
+            log_bb = logarithm_and_reciprocal_of_bb(0)
+            decay_pp(nc.vector, 0)
+            shift_logarithm(nc.vector, 0, log_bb)
+            old_average(nc.gpsimd, 0)
 
             xk_mixed = front.tile([P, PASSES, 4, B], BF16)
             xv_mixed = front.tile([P, PASSES, 4, B], BF16)
@@ -178,35 +211,20 @@ def tile_rwkvtimemix_pa_kernel(
             xk_grouped = front.tile([P, PASSES, B, 4], BF16, align_bytes=64)
             xv_grouped = front.tile([P, PASSES, B, 4], BF16, align_bytes=64)
             for g in range(PASSES):
-                for mixed, grouped in ((xk_mixed, xk_grouped), (xv_mixed, xv_grouped)):
-                    nc.vector.tensor_copy(
-                        out=grouped[:, g].rearrange("p (c i) t -> p c t i", i=4),
-                        in_=mixed[:, g].rearrange("p t (c i) -> p c t i", i=4),
-                    )
-            for g in range(PASSES):
-                for grouped, words, scales in (
-                    (xk_grouped, xk_words, xk_scales), (xv_grouped, xv_words, xv_scales),
-                ):
+                nc.vector.tensor_copy(
+                    out=xk_grouped[:, g].rearrange("p (c i) t -> p c t i", i=4),
+                    in_=xk_mixed[:, g].rearrange("p t (c i) -> p c t i", i=4),
+                )
+                nc.scalar.copy(
+                    out=xv_grouped[:, g].rearrange("p (c i) t -> p c t i", i=4),
+                    in_=xv_mixed[:, g].rearrange("p t (c i) -> p c t i", i=4),
+                )
+            for grouped, words, scales in ((xk_grouped, xk_words, xk_scales), (xv_grouped, xv_words, xv_scales)):
+                for g in range(PASSES):
                     nc.vector.quantize_mx(
                         out=words[:, g, :].bitcast(FP8X4), scales=scales[:, g, :],
                         in_=grouped[:, g].rearrange("p b t -> p (b t)"),
                     )
-
-        logarithm_of_bb(1)
-        reciprocal_of_bb(0)
-
-        def prepare_state(c):
-            cols = slice(c * N_TILE, (c + 1) * N_TILE)
-            for r in range(ROW_TILES):
-                nc.gpsimd.tensor_tensor(
-                    out=decayed[c][:, r, :], in0=pp_sb[:, r, cols], in1=spread[:, A + c * N_TILE : A + (c + 1) * N_TILE],
-                    op=ALU.add,
-                )
-            for r in range(ROW_TILES):
-                nc.gpsimd.tensor_tensor(
-                    out=log_shift[c][:, r, :], in0=log_shift[c][:, r, :], in1=spread[:, cols], op=ALU.subtract
-                )
-                nc.gpsimd.tensor_tensor(out=rho[c][:, r, :], in0=aa_sb[:, r, cols], in1=rho[c][:, r, :], op=ALU.mult)
 
         with tc.tile_pool(name="late", bufs=3) as late:
 
@@ -224,7 +242,7 @@ def tile_rwkvtimemix_pa_kernel(
 
             def output_tile(c, r):
                 rows = slice(r * P, (r + 1) * P)
-                cols = slice(c * N_TILE, (c + 1) * N_TILE)
+                cols = channels(c)
                 k_ps = project(c, r, xk_words, xk_scales, wk_words, wk_scales, "k")
                 v_ps = project(c, r, xv_words, xv_scales, wv_words, wv_scales, "v")
 
@@ -270,16 +288,16 @@ def tile_rwkvtimemix_pa_kernel(
                 )
                 nc.sync.dma_start(out=out_0[rows, cols], in_=wkv[:])
 
-            def prepare_column_tile(c):
-                prepare_state(c)
-                quantise_weight_half(wk_sb[c], wk_words, wk_scales, c)
-                quantise_weight_half(wv_sb[c], wv_words, wv_scales, c)
-
-            prepare_column_tile(0)
-            reciprocal_of_bb(1)
+            quantise_weight_half(wk_sb[0], wk_words, wk_scales, 0)
+            quantise_weight_half(wv_sb[0], wv_words, wv_scales, 0)
+            log_bb = logarithm_and_reciprocal_of_bb(1)
+            decay_pp(nc.gpsimd, 1)
+            shift_logarithm(nc.gpsimd, 1, log_bb)
+            old_average(nc.gpsimd, 1)
             for r in range(ROW_TILES):
                 output_tile(0, r)
                 if r == ROW_TILES // 2 - 1:
-                    prepare_column_tile(1)
+                    quantise_weight_half(wk_sb[1], wk_words, wk_scales, 1)
+                    quantise_weight_half(wv_sb[1], wv_words, wv_scales, 1)
             for r in range(ROW_TILES):
                 output_tile(1, r)

@@ -16,8 +16,9 @@ P = 128
 ROW_TILES = B // P
 K_PASS = 4 * P
 PASSES = H // K_PASS
-N_TILE = 512
-COL_TILES = A // N_TILE
+HALF = A // 2
+HALVES = 2
+TILES_PER_HALF = HALF // P
 PAIR_COLS = 2 * P
 PAIR_BLOCKS = H // PAIR_COLS
 TINY = 2.0 ** -60
@@ -40,133 +41,116 @@ def tile_rwkvtimemix_pa_kernel(
         def rows_on_partitions(dram):
             return dram.rearrange("(r p) n -> p r n", p=P)
 
-        def as_one_row(vector):
-            return vector.rearrange("(o c) -> o c", o=1)
-
-        def channels(c):
-            return slice(c * N_TILE, (c + 1) * N_TILE)
+        def half_channels(c):
+            return slice(c * HALF, (c + 1) * HALF)
 
         mix_rows = const.tile([P, PAIR_COLS], BF16)
         nc.vector.memset(mix_rows[:], 0.0)
-        nc.scalar.dma_start(out=mix_rows[0:4, :], in_=time_mix_k.rearrange("(j c) -> j c", c=PAIR_COLS))
-        nc.scalar.dma_start(out=mix_rows[4:8, :], in_=time_mix_v.rearrange("(j c) -> j c", c=PAIR_COLS))
-        vec_rows = const.tile([P, 2 * A], BF16)
-        nc.vector.memset(vec_rows[:], 0.0)
-        nc.scalar.dma_start(out=vec_rows[0:1, 0:A], in_=as_one_row(time_first))
-        nc.scalar.dma_start(out=vec_rows[1:2, 0:A], in_=as_one_row(time_decay))
-        nc.scalar.dma_start(out=vec_rows[0:1, A : 2 * A], in_=as_one_row(time_decay))
+        nc.sync.dma_start(out=mix_rows[0:4, :], in_=time_mix_k.rearrange("(j c) -> j c", c=PAIR_COLS))
+        nc.sync.dma_start(out=mix_rows[4:8, :], in_=time_mix_v.rearrange("(j c) -> j c", c=PAIR_COLS))
+        channel_rows = const.tile([P, P], BF16)
+        nc.vector.memset(channel_rows[:], 0.0)
+        nc.sync.dma_start(out=channel_rows[0:8, :], in_=time_decay.rearrange("(q m) -> q m", m=P))
+        nc.sync.dma_start(out=channel_rows[8:16, :], in_=time_first.rearrange("(q m) -> q m", m=P))
 
         identity = const.tile([P, P], F32)
         make_identity(nc, identity[:])
-        ones = const.tile([P, P], BF16)
-        nc.vector.memset(ones[:], 1.0)
+        identity_bf16 = const.tile([P, P], BF16)
+        make_identity(nc, identity_bf16[:])
         tiny = const.tile([P, 1], F32)
         nc.vector.memset(tiny[:], TINY)
         mix = const.tile([P, 4 * PAIR_BLOCKS], F32)
         one_minus_mix = const.tile([P, 4 * PAIR_BLOCKS], F32)
-        first_plus_decay = const.tile([P, A], F32)
-        decay = const.tile([P, A], F32)
+        per_channel = const.tile([P, 2 * A // P], F32)
+        half_first_plus_decay = const.tile([P, A // P], F32)
 
         xk_words = keep.tile([P, PASSES, B], U32, align_bytes=64)
         xk_scales = keep.tile([P, PASSES, B], U8, align_bytes=64)
         xv_words = keep.tile([P, PASSES, B], U32, align_bytes=64)
         xv_scales = keep.tile([P, PASSES, B], U8, align_bytes=64)
-        wk_words = keep.tile([P, COL_TILES, PASSES, N_TILE], U32, align_bytes=64)
-        wk_scales = keep.tile([P, COL_TILES, PASSES, N_TILE], U8, align_bytes=64)
-        wv_words = keep.tile([P, COL_TILES, PASSES, N_TILE], U32, align_bytes=64)
-        wv_scales = keep.tile([P, COL_TILES, PASSES, N_TILE], U8, align_bytes=64)
+        wk_words = keep.tile([P, HALVES, PASSES, HALF], U32, align_bytes=64)
+        wk_scales = keep.tile([P, HALVES, PASSES, HALF], U8, align_bytes=64)
+        wv_words = keep.tile([P, HALVES, PASSES, HALF], U32, align_bytes=64)
+        wv_scales = keep.tile([P, HALVES, PASSES, HALF], U8, align_bytes=64)
 
         aa_sb = keep.tile([P, ROW_TILES, A], BF16)
         bb_sb = keep.tile([P, ROW_TILES, A], BF16)
         pp_sb = keep.tile([P, ROW_TILES, A], BF16)
-        log_shift = []
+        aa_bb_t = []
+        pp_t = []
+        log_bb = []
         rho = []
-        decayed = []
-        for c in range(COL_TILES):
-            log_shift.append(keep.tile([P, ROW_TILES, N_TILE], F32, name="log_shift%d" % c))
-            rho.append(keep.tile([P, ROW_TILES, N_TILE], F32, name="rho%d" % c))
-            decayed.append(keep.tile([P, ROW_TILES, N_TILE], F32, name="decayed%d" % c))
+        for c in range(HALVES):
+            aa_bb_t.append(keep.tile([P, TILES_PER_HALF, 2, B], BF16, name="aa_bb_t%d" % c))
+            pp_t.append(keep.tile([P, TILES_PER_HALF, B], BF16, name="pp_t%d" % c))
+            log_bb.append(keep.tile([P, TILES_PER_HALF, B], F32, name="log_bb%d" % c))
+            rho.append(keep.tile([P, TILES_PER_HALF, B], F32, name="rho%d" % c))
 
         def load_state_half(state_sb, state, c):
-            nc.sync.dma_start(out=state_sb[:, :, channels(c)], in_=rows_on_partitions(state)[:, :, channels(c)])
+            nc.sync.dma_start(
+                out=state_sb[:, :, half_channels(c)], in_=rows_on_partitions(state)[:, :, half_channels(c)]
+            )
 
         def load_weight_half(w, c):
-            w_sb = weights.tile([P, N_TILE // P, H], BF16, tag="w_sb")
-            nc.sync.dma_start(out=w_sb[:], in_=rows_on_partitions(w[channels(c), :]))
+            w_sb = weights.tile([P, TILES_PER_HALF, H], BF16, tag="w_sb", bufs=3)
+            nc.sync.dma_start(out=w_sb[:], in_=rows_on_partitions(w[half_channels(c), :]))
             return w_sb
 
         def quantise_weight_half(w_sb, words, scales, c):
             for g in range(PASSES):
-                grouped = weights.tile([P, 4 * N_TILE], BF16, tag="w_grouped", bufs=2, align_bytes=64)
+                grouped = weights.tile([P, 4 * HALF], BF16, tag="w_grouped", align_bytes=64)
                 grouped_pairs = grouped[:].bitcast(F32).rearrange("p (a u) -> p a u", u=2)
-                for half in range(2):
+                for two_tiles in range(TILES_PER_HALF // 2):
                     w_turned = turned.tile([P, 2, 2 * P], F32, tag="turned")
                     for u in range(2):
                         for i in range(2):
-                            block = w_sb[:, 2 * half + i, :].bitcast(F32)
+                            block = w_sb[:, 2 * two_tiles + i, :].bitcast(F32)
                             j = 2 * g + u
                             nc.tensor.transpose(
                                 w_turned[:, u, i * P : (i + 1) * P], block[:, j * P : (j + 1) * P], identity[:]
                             )
                     nc.scalar.copy(
-                        out=grouped_pairs[:, half * 2 * P : (half + 1) * 2 * P, :],
+                        out=grouped_pairs[:, two_tiles * 2 * P : (two_tiles + 1) * 2 * P, :],
                         in_=w_turned[:].rearrange("p u a -> p a u"),
                     )
                 nc.vector.quantize_mx(
                     out=words[:, c, g, :].bitcast(FP8X4), scales=scales[:, c, g, :], in_=grouped[:]
                 )
 
-        def logarithm_and_reciprocal_of_bb(c):
-            log_bb = keep.tile([P, ROW_TILES, N_TILE], F32, tag="log_bb")
-            nc.scalar.activation(out=log_bb[:], in_=bb_sb[:, :, channels(c)], func=ACT.Ln, bias=tiny[:])
-            nc.scalar.activation(out=rho[c][:], in_=log_bb[:], func=ACT.Exp, scale=-1.0)
-            return log_bb
-
-        def decay_pp(engine, c):
-            for r in range(ROW_TILES):
-                engine.tensor_tensor(
-                    out=decayed[c][:, r, :], in0=pp_sb[:, r, channels(c)], in1=decay[:, channels(c)], op=ALU.add
-                )
-
-        def shift_logarithm(engine, c, log_bb):
-            for r in range(ROW_TILES):
-                engine.tensor_tensor(
-                    out=log_shift[c][:, r, :], in0=log_bb[:, r, :], in1=first_plus_decay[:, channels(c)],
-                    op=ALU.subtract,
-                )
-
-        def old_average(engine, c):
-            for r in range(ROW_TILES):
-                engine.tensor_tensor(
-                    out=rho[c][:, r, :], in0=aa_sb[:, r, channels(c)], in1=rho[c][:, r, :], op=ALU.mult
+        def turn_state_half(c):
+            for i in range(TILES_PER_HALF):
+                cols = slice(c * HALF + i * P, c * HALF + (i + 1) * P)
+                aa_bb_ps = turned.tile([P, 2, B], BF16, tag="turned")
+                pp_ps = turned.tile([P, B], BF16, tag="turned")
+                for r in range(ROW_TILES):
+                    rows = slice(r * P, (r + 1) * P)
+                    nc.tensor.transpose(aa_bb_ps[:, 0, rows], aa_sb[:, r, cols], identity_bf16[:])
+                    nc.tensor.transpose(aa_bb_ps[:, 1, rows], bb_sb[:, r, cols], identity_bf16[:])
+                    nc.tensor.transpose(pp_ps[:, rows], pp_sb[:, r, cols], identity_bf16[:])
+                nc.vector.tensor_copy(out=aa_bb_t[c][:, i], in_=aa_bb_ps[:])
+                nc.scalar.copy(out=pp_t[c][:, i, :], in_=pp_ps[:])
+            nc.scalar.activation(out=log_bb[c][:], in_=aa_bb_t[c][:, :, 1, :], func=ACT.Ln, bias=tiny[:])
+            nc.scalar.activation(out=rho[c][:], in_=log_bb[c][:], func=ACT.Exp, scale=-1.0)
+            for i in range(TILES_PER_HALF):
+                nc.gpsimd.tensor_tensor(
+                    out=rho[c][:, i, :], in0=aa_bb_t[c][:, i, 0, :], in1=rho[c][:, i, :], op=ALU.mult
                 )
 
         with tc.tile_pool(name="front", bufs=1) as front:
             x_sb = front.tile([P, ROW_TILES, H], BF16)
             alpha_sb = front.tile([P, ROW_TILES, H], BF16)
-            load_state_half(bb_sb, bb, 0)
-            load_state_half(pp_sb, pp, 0)
             for g in range(PASSES):
                 h_cols = slice(g * K_PASS, (g + 1) * K_PASS)
                 nc.sync.dma_start(out=x_sb[:, :, h_cols], in_=rows_on_partitions(x)[:, :, h_cols])
                 nc.sync.dma_start(out=alpha_sb[:, :, h_cols], in_=rows_on_partitions(alpha)[:, :, h_cols])
-            load_state_half(aa_sb, aa, 0)
-            wk_sb = [load_weight_half(Wk, 0)]
-            wv_sb = [load_weight_half(Wv, 0)]
-            load_state_half(bb_sb, bb, 1)
-            load_state_half(pp_sb, pp, 1)
-            load_state_half(aa_sb, aa, 1)
-            wk_sb.append(load_weight_half(Wk, 1))
-            wv_sb.append(load_weight_half(Wv, 1))
-
-            for c in range(COL_TILES):
-                for first_col, repeated in ((A, decay), (0, first_plus_decay)):
-                    repeated_ps = turned.tile([P, N_TILE], F32, tag="turned")
-                    nc.tensor.matmul(
-                        out=repeated_ps[:], lhsT=ones[:],
-                        rhs=vec_rows[:, first_col + c * N_TILE : first_col + (c + 1) * N_TILE], start=True, stop=True,
-                    )
-                    nc.vector.tensor_copy(out=repeated[:, channels(c)], in_=repeated_ps[:])
+            wk_sb = []
+            wv_sb = []
+            for c in range(HALVES):
+                load_state_half(bb_sb, bb, c)
+                load_state_half(pp_sb, pp, c)
+                load_state_half(aa_sb, aa, c)
+                wk_sb.append(load_weight_half(Wk, c))
+                wv_sb.append(load_weight_half(Wv, c))
 
             mix_turned = turned.tile([P, P], F32, tag="turned")
             nc.tensor.transpose(mix_turned[:], mix_rows[:].bitcast(F32), identity[:])
@@ -174,11 +158,14 @@ def tile_rwkvtimemix_pa_kernel(
             nc.vector.tensor_scalar(
                 out=one_minus_mix[:], in0=mix[:], scalar1=-1.0, scalar2=1.0, op0=ALU.mult, op1=ALU.add
             )
-
-            log_bb = logarithm_and_reciprocal_of_bb(0)
-            decay_pp(nc.vector, 0)
-            shift_logarithm(nc.vector, 0, log_bb)
-            old_average(nc.gpsimd, 0)
+            channel_turned = turned.tile([P, P], BF16, tag="turned")
+            nc.tensor.transpose(channel_turned[:], channel_rows[:], identity_bf16[:])
+            nc.vector.tensor_copy(out=per_channel[:], in_=channel_turned[:, 0 : 2 * A // P])
+            nc.vector.tensor_tensor(
+                out=half_first_plus_decay[:], in0=per_channel[:, 0 : A // P], in1=per_channel[:, A // P : 2 * A // P],
+                op=ALU.add,
+            )
+            nc.vector.tensor_scalar_mul(out=half_first_plus_decay[:], in0=half_first_plus_decay[:], scalar1=0.5)
 
             xk_mixed = front.tile([P, PASSES, 4, B], BF16)
             xv_mixed = front.tile([P, PASSES, 4, B], BF16)
@@ -196,29 +183,25 @@ def tile_rwkvtimemix_pa_kernel(
                 x_pairs = x_turned[:].bitcast(BF16).rearrange("p (b e) -> p b e", e=2)
                 alpha_pairs = alpha_turned[:].bitcast(BF16).rearrange("p (b e) -> p b e", e=2)
                 for e in range(2):
-                    for first_col, mixed in ((0, xk_mixed), (2 * PAIR_BLOCKS, xv_mixed)):
-                        col = first_col + 2 * j + e
+                    for mix_col, mixed in ((2 * j + e, xk_mixed), (2 * PAIR_BLOCKS + 2 * j + e, xv_mixed)):
                         alpha_part = front.tile([P, B], F32, tag="alpha_part", bufs=4)
                         nc.scalar.activation(
                             out=alpha_part[:], in_=alpha_pairs[:, :, e], func=ACT.Copy,
-                            scale=one_minus_mix[:, col : col + 1],
+                            scale=one_minus_mix[:, mix_col : mix_col + 1],
                         )
                         nc.vector.scalar_tensor_tensor(
-                            out=mixed[:, g, 2 * u + e, :], in0=x_pairs[:, :, e], scalar=mix[:, col : col + 1],
+                            out=mixed[:, g, 2 * u + e, :], in0=x_pairs[:, :, e], scalar=mix[:, mix_col : mix_col + 1],
                             in1=alpha_part[:], op0=ALU.mult, op1=ALU.add,
                         )
 
             xk_grouped = front.tile([P, PASSES, B, 4], BF16, align_bytes=64)
             xv_grouped = front.tile([P, PASSES, B, 4], BF16, align_bytes=64)
             for g in range(PASSES):
-                nc.vector.tensor_copy(
-                    out=xk_grouped[:, g].rearrange("p (c i) t -> p c t i", i=4),
-                    in_=xk_mixed[:, g].rearrange("p t (c i) -> p c t i", i=4),
-                )
-                nc.scalar.copy(
-                    out=xv_grouped[:, g].rearrange("p (c i) t -> p c t i", i=4),
-                    in_=xv_mixed[:, g].rearrange("p t (c i) -> p c t i", i=4),
-                )
+                for mixed, grouped in ((xk_mixed, xk_grouped), (xv_mixed, xv_grouped)):
+                    nc.vector.tensor_copy(
+                        out=grouped[:, g].rearrange("p (c i) t -> p c t i", i=4),
+                        in_=mixed[:, g].rearrange("p t (c i) -> p c t i", i=4),
+                    )
             for grouped, words, scales in ((xk_grouped, xk_words, xk_scales), (xv_grouped, xv_words, xv_scales)):
                 for g in range(PASSES):
                     nc.vector.quantize_mx(
@@ -228,76 +211,102 @@ def tile_rwkvtimemix_pa_kernel(
 
         with tc.tile_pool(name="late", bufs=3) as late:
 
-            def project(c, r, x_words, x_scales, w_words, w_scales, tag):
-                acc = sums.tile([P, N_TILE], F32, tag=tag)
-                rows = slice(r * P, (r + 1) * P)
+            def project(c, i, w_words, w_scales, x_words, x_scales, tag):
+                acc = sums.tile([P, B], F32, tag=tag)
+                cols = slice(i * P, (i + 1) * P)
                 for g in range(PASSES):
                     nc.tensor.matmul_mx(
                         out=acc[:],
-                        lhsT=x_words[:, g, rows].bitcast(FP8X4), lhsT_scale=x_scales[:, g, rows],
-                        rhs=w_words[:, c, g, :].bitcast(FP8X4), rhs_scale=w_scales[:, c, g, :],
+                        lhsT=w_words[:, c, g, cols].bitcast(FP8X4), lhsT_scale=w_scales[:, c, g, cols],
+                        rhs=x_words[:, g, :].bitcast(FP8X4), rhs_scale=x_scales[:, g, :],
                         start=(g == 0), stop=(g == PASSES - 1),
                     )
                 return acc
 
-            def output_tile(c, r):
-                rows = slice(r * P, (r + 1) * P)
-                cols = channels(c)
-                k_ps = project(c, r, xk_words, xk_scales, wk_words, wk_scales, "k")
-                v_ps = project(c, r, xv_words, xv_scales, wv_words, wv_scales, "v")
+            def turn_back(parts):
+                back = turned.tile([P, ROW_TILES, P], F32, tag="turned")
+                for r in range(ROW_TILES):
+                    for n, part in enumerate(parts):
+                        nc.tensor.matmul(
+                            out=back[:, r, :], lhsT=part[:, r * P : (r + 1) * P], rhs=identity[:],
+                            is_transpose=True, start=(n == 0), stop=(n == len(parts) - 1),
+                        )
+                return back
 
-                d2 = late.tile([P, N_TILE], F32, tag="d2")
-                nc.vector.tensor_tensor(out=d2[:], in0=k_ps[:], in1=decayed[c][:, r, :], op=ALU.subtract)
-                qq2 = late.tile([P, N_TILE], F32, tag="qq2")
-                nc.vector.tensor_tensor(out=qq2[:], in0=k_ps[:], in1=decayed[c][:, r, :], op=ALU.max)
-                nc.sync.dma_start(out=out_3[rows, cols], in_=qq2[:])
-                wkv = late.tile([P, N_TILE], F32, tag="wkv")
-                nc.vector.tensor_tensor(out=wkv[:], in0=v_ps[:], in1=rho[c][:, r, :], op=ALU.subtract)
-                gate = late.tile([P, N_TILE], F32, tag="gate")
-                nc.vector.tensor_tensor(out=gate[:], in0=d2[:], in1=log_shift[c][:, r, :], op=ALU.subtract)
+            def store(out, result, c, i):
+                cols = slice(c * HALF + i * P, c * HALF + (i + 1) * P)
+                nc.sync.dma_start(out=rows_on_partitions(out)[:, :, cols], in_=result[:])
 
-                grow_old = late.tile([P, N_TILE], F32, tag="grow_old")
+            def channel_tile(c, i):
+                q = c * TILES_PER_HALF + i
+                decay = per_channel[:, q : q + 1]
+                aa_t = aa_bb_t[c][:, i, 0, :]
+                bb_t = aa_bb_t[c][:, i, 1, :]
+                k_ps = project(c, i, wk_words, wk_scales, xk_words, xk_scales, "k")
+                v_ps = project(c, i, wv_words, wv_scales, xv_words, xv_scales, "v")
+
+                d2 = late.tile([P, B], F32, tag="d2")
+                nc.vector.scalar_tensor_tensor(
+                    out=d2[:], in0=k_ps[:], scalar=decay, in1=pp_t[c][:, i, :], op0=ALU.subtract, op1=ALU.subtract
+                )
+                qq2_t = late.tile([P, B], F32, tag="qq2_t")
+                nc.vector.scalar_tensor_tensor(
+                    out=qq2_t[:], in0=pp_t[c][:, i, :], scalar=decay, in1=k_ps[:], op0=ALU.add, op1=ALU.max
+                )
+                moved = late.tile([P, B], F32, tag="moved")
+                nc.vector.tensor_tensor(out=moved[:], in0=v_ps[:], in1=rho[c][:, i, :], op=ALU.subtract)
+                gate = late.tile([P, B], F32, tag="gate")
+                nc.gpsimd.tensor_tensor(out=gate[:], in0=d2[:], in1=log_bb[c][:, i, :], op=ALU.subtract)
+
+                grow_old = late.tile([P, B], F32, tag="grow_old")
                 nc.scalar.activation(out=grow_old[:], in_=d2[:], func=ACT.Exp, scale=-1.0)
-                grow_new = late.tile([P, N_TILE], F32, tag="grow_new")
+                grow_new = late.tile([P, B], F32, tag="grow_new")
                 nc.scalar.activation(out=grow_new[:], in_=d2[:], func=ACT.Exp)
-                nc.scalar.activation(out=gate[:], in_=gate[:], func=ACT.Tanh, scale=0.5)
+                nc.scalar.activation(
+                    out=gate[:], in_=gate[:], func=ACT.Tanh, scale=0.5, bias=half_first_plus_decay[:, q : q + 1]
+                )
 
-                new_part = late.tile([P, N_TILE], F32, tag="new_part")
+                new_part = late.tile([P, B], F32, tag="new_part")
                 nc.vector.scalar_tensor_tensor(
                     out=new_part[:], in0=grow_new[:], scalar=1.0, in1=v_ps[:], op0=ALU.min, op1=ALU.mult
                 )
-                next_aa = late.tile([P, N_TILE], F32, tag="next_aa")
+                old_part = late.tile([P, B], F32, tag="old_part")
                 nc.vector.scalar_tensor_tensor(
-                    out=next_aa[:], in0=grow_old[:], scalar=1.0, in1=aa_sb[:, r, cols], op0=ALU.min, op1=ALU.mult
+                    out=old_part[:], in0=grow_old[:], scalar=1.0, in1=aa_t, op0=ALU.min, op1=ALU.mult
                 )
-                next_bb = late.tile([P, N_TILE], F32, tag="next_bb")
+                next_bb_t = late.tile([P, B], F32, tag="next_bb_t")
                 nc.vector.scalar_tensor_tensor(
-                    out=next_bb[:], in0=grow_old[:], scalar=1.0, in1=bb_sb[:, r, cols], op0=ALU.min, op1=ALU.mult
+                    out=next_bb_t[:], in0=grow_old[:], scalar=1.0, in1=bb_t, op0=ALU.min, op1=ALU.mult
                 )
                 nc.vector.scalar_tensor_tensor(
-                    out=wkv[:], in0=gate[:], scalar=1.0, in1=wkv[:], op0=ALU.add, op1=ALU.mult
+                    out=moved[:], in0=gate[:], scalar=1.0, in1=moved[:], op0=ALU.add, op1=ALU.mult
                 )
-                nc.vector.tensor_tensor(out=next_aa[:], in0=next_aa[:], in1=new_part[:], op=ALU.add)
-                nc.sync.dma_start(out=out_1[rows, cols], in_=next_aa[:])
                 nc.vector.scalar_tensor_tensor(
-                    out=next_bb[:], in0=grow_new[:], scalar=1.0, in1=next_bb[:], op0=ALU.min, op1=ALU.add
+                    out=next_bb_t[:], in0=grow_new[:], scalar=1.0, in1=next_bb_t[:], op0=ALU.min, op1=ALU.add
                 )
-                nc.sync.dma_start(out=out_2[rows, cols], in_=next_bb[:])
-                nc.vector.scalar_tensor_tensor(
-                    out=wkv[:], in0=wkv[:], scalar=0.5, in1=rho[c][:, r, :], op0=ALU.mult, op1=ALU.add
-                )
-                nc.sync.dma_start(out=out_0[rows, cols], in_=wkv[:])
+
+                qq2 = late.tile([P, ROW_TILES, P], F32, tag="qq2", bufs=2)
+                nc.vector.tensor_copy(out=qq2[:], in_=turn_back([qq2_t])[:])
+                store(out_3, qq2, c, i)
+                next_aa = late.tile([P, ROW_TILES, P], F32, tag="next_aa", bufs=2)
+                nc.scalar.copy(out=next_aa[:], in_=turn_back([old_part, new_part])[:])
+                store(out_1, next_aa, c, i)
+                next_bb = late.tile([P, ROW_TILES, P], F32, tag="next_bb", bufs=2)
+                nc.scalar.copy(out=next_bb[:], in_=turn_back([next_bb_t])[:])
+                store(out_2, next_bb, c, i)
+                wkv = late.tile([P, ROW_TILES, P], F32, tag="wkv", bufs=2)
+                nc.scalar.mul(out=wkv[:], in_=turn_back([moved, rho[c][:, i, :], rho[c][:, i, :]])[:], mul=0.5)
+                store(out_0, wkv, c, i)
 
             quantise_weight_half(wk_sb[0], wk_words, wk_scales, 0)
             quantise_weight_half(wv_sb[0], wv_words, wv_scales, 0)
-            log_bb = logarithm_and_reciprocal_of_bb(1)
-            decay_pp(nc.gpsimd, 1)
-            shift_logarithm(nc.gpsimd, 1, log_bb)
-            old_average(nc.gpsimd, 1)
-            for r in range(ROW_TILES):
-                output_tile(0, r)
-                if r == ROW_TILES // 2 - 1:
+            turn_state_half(0)
+            for i in range(TILES_PER_HALF):
+                channel_tile(0, i)
+                if i == 0:
+                    turn_state_half(1)
+                if i == 1:
                     quantise_weight_half(wk_sb[1], wk_words, wk_scales, 1)
                     quantise_weight_half(wv_sb[1], wv_words, wv_scales, 1)
-            for r in range(ROW_TILES):
-                output_tile(1, r)
+            for i in range(TILES_PER_HALF):
+                channel_tile(1, i)

from contextlib import ExitStack

import concourse.mybir as mybir
from concourse.masks import make_identity

F32 = mybir.dt.float32
BF16 = mybir.dt.bfloat16
U32 = mybir.dt.uint32
U8 = mybir.dt.uint8
FP8X4 = mybir.dt.float8_e4m3fn_x4
ALU = mybir.AluOpType
ACT = mybir.ActivationFunctionType

B, H, A = 512, 1024, 1024
P = 128
ROW_TILES = B // P
K_PASS = 4 * P
PASSES = H // K_PASS
HALF = A // 2
HALVES = 2
TILES_PER_HALF = HALF // P
PAIR_COLS = 2 * P
PAIR_BLOCKS = H // PAIR_COLS
TINY = 2.0 ** -60

FLOPS = 2 * 2 * B * H * A


def tile_rwkvtimemix_pa_kernel(
    tc, x, alpha, aa, bb, pp, time_decay, time_first, time_mix_k, time_mix_v, Wk, Wv,
    out_0, out_1, out_2, out_3,
):
    nc = tc.nc
    with ExitStack() as stack:
        const = stack.enter_context(tc.tile_pool(name="const", bufs=1))
        keep = stack.enter_context(tc.tile_pool(name="keep", bufs=1))
        weights = stack.enter_context(tc.tile_pool(name="weights", bufs=4))
        turned = stack.enter_context(tc.psum_pool(name="turned", bufs=4))
        sums = stack.enter_context(tc.psum_pool(name="sums", bufs=2))

        def rows_on_partitions(dram):
            return dram.rearrange("(r p) n -> p r n", p=P)

        def half_channels(c):
            return slice(c * HALF, (c + 1) * HALF)

        mix_rows = const.tile([P, PAIR_COLS], BF16)
        nc.vector.memset(mix_rows[:], 0.0)
        nc.sync.dma_start(out=mix_rows[0:4, :], in_=time_mix_k.rearrange("(j c) -> j c", c=PAIR_COLS))
        nc.sync.dma_start(out=mix_rows[4:8, :], in_=time_mix_v.rearrange("(j c) -> j c", c=PAIR_COLS))
        channel_rows = const.tile([P, P], BF16)
        nc.vector.memset(channel_rows[:], 0.0)
        nc.sync.dma_start(out=channel_rows[0:8, :], in_=time_decay.rearrange("(q m) -> q m", m=P))
        nc.sync.dma_start(out=channel_rows[8:16, :], in_=time_first.rearrange("(q m) -> q m", m=P))

        identity = const.tile([P, P], F32)
        make_identity(nc, identity[:])
        identity_bf16 = const.tile([P, P], BF16)
        make_identity(nc, identity_bf16[:])
        tiny = const.tile([P, 1], F32)
        nc.vector.memset(tiny[:], TINY)
        mix = const.tile([P, 4 * PAIR_BLOCKS], F32)
        one_minus_mix = const.tile([P, 4 * PAIR_BLOCKS], F32)
        per_channel = const.tile([P, 2 * A // P], F32)
        half_first_plus_decay = const.tile([P, A // P], F32)

        xk_words = keep.tile([P, PASSES, B], U32, align_bytes=64)
        xk_scales = keep.tile([P, PASSES, B], U8, align_bytes=64)
        xv_words = keep.tile([P, PASSES, B], U32, align_bytes=64)
        xv_scales = keep.tile([P, PASSES, B], U8, align_bytes=64)
        wk_words = keep.tile([P, HALVES, PASSES, HALF], U32, align_bytes=64)
        wk_scales = keep.tile([P, HALVES, PASSES, HALF], U8, align_bytes=64)
        wv_words = keep.tile([P, HALVES, PASSES, HALF], U32, align_bytes=64)
        wv_scales = keep.tile([P, HALVES, PASSES, HALF], U8, align_bytes=64)

        aa_sb = keep.tile([P, ROW_TILES, A], BF16)
        bb_sb = keep.tile([P, ROW_TILES, A], BF16)
        pp_sb = keep.tile([P, ROW_TILES, A], BF16)
        aa_bb_t = []
        pp_t = []
        log_bb = []
        rho = []
        for c in range(HALVES):
            aa_bb_t.append(keep.tile([P, TILES_PER_HALF, 2, B], BF16, name="aa_bb_t%d" % c))
            pp_t.append(keep.tile([P, TILES_PER_HALF, B], BF16, name="pp_t%d" % c))
            log_bb.append(keep.tile([P, TILES_PER_HALF, B], F32, name="log_bb%d" % c))
            rho.append(keep.tile([P, TILES_PER_HALF, B], F32, name="rho%d" % c))

        def load_state_half(state_sb, state, c):
            nc.sync.dma_start(
                out=state_sb[:, :, half_channels(c)], in_=rows_on_partitions(state)[:, :, half_channels(c)]
            )

        def load_weight_half(w, c):
            w_sb = weights.tile([P, TILES_PER_HALF, H], BF16, tag="w_sb", bufs=3)
            nc.sync.dma_start(out=w_sb[:], in_=rows_on_partitions(w[half_channels(c), :]))
            return w_sb

        def quantise_weight_half(w_sb, words, scales, c):
            for g in range(PASSES):
                grouped = weights.tile([P, 4 * HALF], BF16, tag="w_grouped", align_bytes=64)
                grouped_pairs = grouped[:].bitcast(F32).rearrange("p (a u) -> p a u", u=2)
                for two_tiles in range(TILES_PER_HALF // 2):
                    w_turned = turned.tile([P, 2, 2 * P], F32, tag="turned")
                    for u in range(2):
                        for i in range(2):
                            block = w_sb[:, 2 * two_tiles + i, :].bitcast(F32)
                            j = 2 * g + u
                            nc.tensor.transpose(
                                w_turned[:, u, i * P : (i + 1) * P], block[:, j * P : (j + 1) * P], identity[:]
                            )
                    nc.scalar.copy(
                        out=grouped_pairs[:, two_tiles * 2 * P : (two_tiles + 1) * 2 * P, :],
                        in_=w_turned[:].rearrange("p u a -> p a u"),
                    )
                nc.vector.quantize_mx(
                    out=words[:, c, g, :].bitcast(FP8X4), scales=scales[:, c, g, :], in_=grouped[:]
                )

        def turn_state_half(c):
            for i in range(TILES_PER_HALF):
                cols = slice(c * HALF + i * P, c * HALF + (i + 1) * P)
                aa_bb_ps = turned.tile([P, 2, B], BF16, tag="turned")
                pp_ps = turned.tile([P, B], BF16, tag="turned")
                for r in range(ROW_TILES):
                    rows = slice(r * P, (r + 1) * P)
                    nc.tensor.transpose(aa_bb_ps[:, 0, rows], aa_sb[:, r, cols], identity_bf16[:])
                    nc.tensor.transpose(aa_bb_ps[:, 1, rows], bb_sb[:, r, cols], identity_bf16[:])
                    nc.tensor.transpose(pp_ps[:, rows], pp_sb[:, r, cols], identity_bf16[:])
                nc.vector.tensor_copy(out=aa_bb_t[c][:, i], in_=aa_bb_ps[:])
                nc.scalar.copy(out=pp_t[c][:, i, :], in_=pp_ps[:])
            nc.scalar.activation(out=log_bb[c][:], in_=aa_bb_t[c][:, :, 1, :], func=ACT.Ln, bias=tiny[:])
            nc.scalar.activation(out=rho[c][:], in_=log_bb[c][:], func=ACT.Exp, scale=-1.0)
            for i in range(TILES_PER_HALF):
                nc.gpsimd.tensor_tensor(
                    out=rho[c][:, i, :], in0=aa_bb_t[c][:, i, 0, :], in1=rho[c][:, i, :], op=ALU.mult
                )

        with tc.tile_pool(name="front", bufs=1) as front:
            x_sb = front.tile([P, ROW_TILES, H], BF16)
            alpha_sb = front.tile([P, ROW_TILES, H], BF16)
            for g in range(PASSES):
                h_cols = slice(g * K_PASS, (g + 1) * K_PASS)
                nc.sync.dma_start(out=x_sb[:, :, h_cols], in_=rows_on_partitions(x)[:, :, h_cols])
                nc.sync.dma_start(out=alpha_sb[:, :, h_cols], in_=rows_on_partitions(alpha)[:, :, h_cols])
            wk_sb = []
            wv_sb = []
            for c in range(HALVES):
                load_state_half(bb_sb, bb, c)
                load_state_half(pp_sb, pp, c)
                load_state_half(aa_sb, aa, c)
                wk_sb.append(load_weight_half(Wk, c))
                wv_sb.append(load_weight_half(Wv, c))

            mix_turned = turned.tile([P, P], F32, tag="turned")
            nc.tensor.transpose(mix_turned[:], mix_rows[:].bitcast(F32), identity[:])
            nc.vector.tensor_copy(out=mix[:], in_=mix_turned[:, 0 : 2 * PAIR_BLOCKS].bitcast(BF16))
            nc.vector.tensor_scalar(
                out=one_minus_mix[:], in0=mix[:], scalar1=-1.0, scalar2=1.0, op0=ALU.mult, op1=ALU.add
            )
            channel_turned = turned.tile([P, P], BF16, tag="turned")
            nc.tensor.transpose(channel_turned[:], channel_rows[:], identity_bf16[:])
            nc.vector.tensor_copy(out=per_channel[:], in_=channel_turned[:, 0 : 2 * A // P])
            nc.vector.tensor_tensor(
                out=half_first_plus_decay[:], in0=per_channel[:, 0 : A // P], in1=per_channel[:, A // P : 2 * A // P],
                op=ALU.add,
            )
            nc.vector.tensor_scalar_mul(out=half_first_plus_decay[:], in0=half_first_plus_decay[:], scalar1=0.5)

            xk_mixed = front.tile([P, PASSES, 4, B], BF16)
            xv_mixed = front.tile([P, PASSES, 4, B], BF16)
            for j in range(PAIR_BLOCKS):
                g, u = divmod(j, 2)
                x_turned = turned.tile([P, B], F32, tag="turned")
                alpha_turned = turned.tile([P, B], F32, tag="turned")
                for r in range(ROW_TILES):
                    rows = slice(r * P, (r + 1) * P)
                    pair_cols = slice(j * P, (j + 1) * P)
                    nc.tensor.transpose(x_turned[:, rows], x_sb[:, r, :].bitcast(F32)[:, pair_cols], identity[:])
                    nc.tensor.transpose(
                        alpha_turned[:, rows], alpha_sb[:, r, :].bitcast(F32)[:, pair_cols], identity[:]
                    )
                x_pairs = x_turned[:].bitcast(BF16).rearrange("p (b e) -> p b e", e=2)
                alpha_pairs = alpha_turned[:].bitcast(BF16).rearrange("p (b e) -> p b e", e=2)
                for e in range(2):
                    for mix_col, mixed in ((2 * j + e, xk_mixed), (2 * PAIR_BLOCKS + 2 * j + e, xv_mixed)):
                        alpha_part = front.tile([P, B], F32, tag="alpha_part", bufs=4)
                        nc.scalar.activation(
                            out=alpha_part[:], in_=alpha_pairs[:, :, e], func=ACT.Copy,
                            scale=one_minus_mix[:, mix_col : mix_col + 1],
                        )
                        nc.vector.scalar_tensor_tensor(
                            out=mixed[:, g, 2 * u + e, :], in0=x_pairs[:, :, e], scalar=mix[:, mix_col : mix_col + 1],
                            in1=alpha_part[:], op0=ALU.mult, op1=ALU.add,
                        )

            xk_grouped = front.tile([P, PASSES, B, 4], BF16, align_bytes=64)
            xv_grouped = front.tile([P, PASSES, B, 4], BF16, align_bytes=64)
            for g in range(PASSES):
                for mixed, grouped in ((xk_mixed, xk_grouped), (xv_mixed, xv_grouped)):
                    nc.vector.tensor_copy(
                        out=grouped[:, g].rearrange("p (c i) t -> p c t i", i=4),
                        in_=mixed[:, g].rearrange("p t (c i) -> p c t i", i=4),
                    )
            for grouped, words, scales in ((xk_grouped, xk_words, xk_scales), (xv_grouped, xv_words, xv_scales)):
                for g in range(PASSES):
                    nc.vector.quantize_mx(
                        out=words[:, g, :].bitcast(FP8X4), scales=scales[:, g, :],
                        in_=grouped[:, g].rearrange("p b t -> p (b t)"),
                    )

        with tc.tile_pool(name="late", bufs=3) as late:

            def project(c, i, w_words, w_scales, x_words, x_scales, tag):
                acc = sums.tile([P, B], F32, tag=tag)
                cols = slice(i * P, (i + 1) * P)
                for g in range(PASSES):
                    nc.tensor.matmul_mx(
                        out=acc[:],
                        lhsT=w_words[:, c, g, cols].bitcast(FP8X4), lhsT_scale=w_scales[:, c, g, cols],
                        rhs=x_words[:, g, :].bitcast(FP8X4), rhs_scale=x_scales[:, g, :],
                        start=(g == 0), stop=(g == PASSES - 1),
                    )
                return acc

            def turn_back(parts):
                back = turned.tile([P, ROW_TILES, P], F32, tag="turned")
                for r in range(ROW_TILES):
                    for n, part in enumerate(parts):
                        nc.tensor.matmul(
                            out=back[:, r, :], lhsT=part[:, r * P : (r + 1) * P], rhs=identity[:],
                            is_transpose=True, start=(n == 0), stop=(n == len(parts) - 1),
                        )
                return back

            def store(out, result, c, i):
                cols = slice(c * HALF + i * P, c * HALF + (i + 1) * P)
                nc.sync.dma_start(out=rows_on_partitions(out)[:, :, cols], in_=result[:])

            def channel_tile(c, i):
                q = c * TILES_PER_HALF + i
                decay = per_channel[:, q : q + 1]
                aa_t = aa_bb_t[c][:, i, 0, :]
                bb_t = aa_bb_t[c][:, i, 1, :]
                k_ps = project(c, i, wk_words, wk_scales, xk_words, xk_scales, "k")
                v_ps = project(c, i, wv_words, wv_scales, xv_words, xv_scales, "v")

                d2 = late.tile([P, B], F32, tag="d2")
                nc.vector.scalar_tensor_tensor(
                    out=d2[:], in0=k_ps[:], scalar=decay, in1=pp_t[c][:, i, :], op0=ALU.subtract, op1=ALU.subtract
                )
                qq2_t = late.tile([P, B], F32, tag="qq2_t")
                nc.vector.scalar_tensor_tensor(
                    out=qq2_t[:], in0=pp_t[c][:, i, :], scalar=decay, in1=k_ps[:], op0=ALU.add, op1=ALU.max
                )
                moved = late.tile([P, B], F32, tag="moved")
                nc.vector.tensor_tensor(out=moved[:], in0=v_ps[:], in1=rho[c][:, i, :], op=ALU.subtract)
                gate = late.tile([P, B], F32, tag="gate")
                nc.gpsimd.tensor_tensor(out=gate[:], in0=d2[:], in1=log_bb[c][:, i, :], op=ALU.subtract)

                grow_old = late.tile([P, B], F32, tag="grow_old")
                nc.scalar.activation(out=grow_old[:], in_=d2[:], func=ACT.Exp, scale=-1.0)
                grow_new = late.tile([P, B], F32, tag="grow_new")
                nc.scalar.activation(out=grow_new[:], in_=d2[:], func=ACT.Exp)
                nc.scalar.activation(
                    out=gate[:], in_=gate[:], func=ACT.Tanh, scale=0.5, bias=half_first_plus_decay[:, q : q + 1]
                )

                new_part = late.tile([P, B], F32, tag="new_part")
                nc.vector.scalar_tensor_tensor(
                    out=new_part[:], in0=grow_new[:], scalar=1.0, in1=v_ps[:], op0=ALU.min, op1=ALU.mult
                )
                old_part = late.tile([P, B], F32, tag="old_part")
                nc.vector.scalar_tensor_tensor(
                    out=old_part[:], in0=grow_old[:], scalar=1.0, in1=aa_t, op0=ALU.min, op1=ALU.mult
                )
                next_bb_t = late.tile([P, B], F32, tag="next_bb_t")
                nc.vector.scalar_tensor_tensor(
                    out=next_bb_t[:], in0=grow_old[:], scalar=1.0, in1=bb_t, op0=ALU.min, op1=ALU.mult
                )
                nc.vector.scalar_tensor_tensor(
                    out=moved[:], in0=gate[:], scalar=1.0, in1=moved[:], op0=ALU.add, op1=ALU.mult
                )
                nc.vector.scalar_tensor_tensor(
                    out=next_bb_t[:], in0=grow_new[:], scalar=1.0, in1=next_bb_t[:], op0=ALU.min, op1=ALU.add
                )

                qq2 = late.tile([P, ROW_TILES, P], F32, tag="qq2", bufs=2)
                nc.vector.tensor_copy(out=qq2[:], in_=turn_back([qq2_t])[:])
                store(out_3, qq2, c, i)
                next_aa = late.tile([P, ROW_TILES, P], F32, tag="next_aa", bufs=2)
                nc.scalar.copy(out=next_aa[:], in_=turn_back([old_part, new_part])[:])
                store(out_1, next_aa, c, i)
                next_bb = late.tile([P, ROW_TILES, P], F32, tag="next_bb", bufs=2)
                nc.scalar.copy(out=next_bb[:], in_=turn_back([next_bb_t])[:])
                store(out_2, next_bb, c, i)
                wkv = late.tile([P, ROW_TILES, P], F32, tag="wkv", bufs=2)
                nc.scalar.mul(out=wkv[:], in_=turn_back([moved, rho[c][:, i, :], rho[c][:, i, :]])[:], mul=0.5)
                store(out_0, wkv, c, i)

            quantise_weight_half(wk_sb[0], wk_words, wk_scales, 0)
            quantise_weight_half(wv_sb[0], wv_words, wv_scales, 0)
            turn_state_half(0)
            for i in range(TILES_PER_HALF):
                channel_tile(0, i)
                if i == 0:
                    turn_state_half(1)
                if i == 1:
                    quantise_weight_half(wk_sb[1], wk_words, wk_scales, 1)
                    quantise_weight_half(wv_sb[1], wv_words, wv_scales, 1)
            for i in range(TILES_PER_HALF):
                channel_tile(1, i)
